import numpy as np
import ml_dtypes


def mxq(x, axis, fmt="e4m3"):
    dtype, down = {"e4m3": (ml_dtypes.float8_e4m3fn, 7), "e5m2": (ml_dtypes.float8_e5m2, 14)}[fmt]
    v = np.moveaxis(np.asarray(x, np.float32).astype(ml_dtypes.bfloat16).astype(np.float64), axis, -1)
    blocks = v.reshape(v.shape[:-1] + (-1, 32))
    amax = np.abs(blocks).max(-1, keepdims=True)
    byte = np.maximum(np.where(amax > 0, np.frexp(amax)[1] - 1 + 127, 0) - down, 1)
    scale = np.exp2(byte - 127.0)
    codes = (blocks / scale).astype(np.float32).astype(dtype).astype(np.float64)
    return np.moveaxis((codes * scale).reshape(v.shape), -1, axis)


WIDE = False


def mx_kscale(k):
    if not WIDE:
        return np.ones(k)
    levels = np.array([10, -10, 5, -5, 0])
    if k % 512:
        return np.exp2(np.random.permutation(np.resize(levels, k // 32))).repeat(32)
    a = np.empty((k // 512, 16))
    for p in range(k // 512):
        a[p, :8] = np.random.permutation(np.resize(levels, 8))
        for g in range(8):
            far = levels[np.abs(levels - a[p, g]) >= 10]
            a[p, g + 8] = far[np.random.randint(len(far))]
    return np.exp2(a.ravel()).repeat(32)


BF16 = ml_dtypes.bfloat16


def bf(x):
    return np.asarray(x, np.float32).astype(BF16)


def f64(x):
    return np.asarray(x).astype(np.float64)


B, N, D, H, DK, P = 4, 2048, 512, 2, 128, 512
E = H * DK


def draw0():
    s = mx_kscale(D)
    return {"Q": bf(np.random.standard_normal((B, N, D)) * s),
            "WQ": bf(np.random.standard_normal((E, D)) * 1.5 / np.sqrt(D) / s)}


def core(Q, WQ):
    q = mxq(f64(Q), 2, "e4m3") @ mxq(f64(WQ), 1, "e4m3").T
    q = q.reshape(B, N, H, DK).transpose(0, 2, 1, 3)
    g = np.exp(q - q.max(-1, keepdims=True))
    return g / g.sum(-1, keepdims=True)


def e4m3fn_bytes(y):
    return np.clip(np.asarray(y, np.float64), -448.0, 448.0).astype(np.float32).astype(ml_dtypes.float8_e4m3fn).view(np.uint8)


def e4m3fn_values(b):
    return np.asarray(b, np.uint8).view(ml_dtypes.float8_e4m3fn).astype(np.float64)


def setup_inputs():
    d = draw0()
    x0 = np.asarray(d['Q']).astype(np.float64)
    s = (np.max(np.abs(x0), axis=(0, 1), keepdims=True) / 448.0).astype(np.float32)
    out = {}
    for k, v in d.items():
        if k == 'Q':
            out['Q_bytes'] = e4m3fn_bytes(x0 / s.astype(np.float64))
            out['Q_scale'] = s
        else:
            out[k] = v
    return out


def reference(Q_bytes, Q_scale, WQ):
    return core(e4m3fn_values(Q_bytes) * Q_scale.astype(np.float64), WQ)

@@ -1,0 +1,336 @@
+from contextlib import ExitStack
+
+import concourse.mybir as mybir
+from concourse.masks import make_identity
+
+FLOPS = 2 * 8192 * 512 * 256
+
+F32 = mybir.dt.float32
+BF16 = mybir.dt.bfloat16
+U32 = mybir.dt.uint32
+U8 = mybir.dt.uint8
+FP8 = mybir.dt.float8_e4m3fn
+FP8X4 = mybir.dt.float8_e4m3fn_x4
+ACT = mybir.ActivationFunctionType
+ALU = mybir.AluOpType
+AX = mybir.AxisListType
+
+P = 128
+K = 512
+BATCH = 4
+HEADS = 2
+DK = 128
+LOADS = 16
+UNITS = 32
+UW = 2 * K
+
+GROUPS = (
+    [[u] for u in range(3, 6)]
+    + [[u, u + 1] for u in range(6, UNITS - 2, 2)]
+    + [[UNITS - 2], [UNITS - 1], [0], [1], [2]]
+)
+EARLY = (len(GROUPS) - 3, len(GROUPS) - 2, len(GROUPS) - 1)
+WEAVE_STEPS = (4, 5, 6, 7, 8, 9)
+POOL_SHARE = {1: (3,), 2: (0, 3, 6)}
+TAIL_GROUPS = 7
+TAIL_VECTOR = (1, 2, 4, 5, 7)
+WARM_MATMULS = 4
+
+
+def tile_multiheadattention_pb_t_kernel(tc, Q_bytes, Q_scale, WQ, out):
+    nc = tc.nc
+    n_groups = len(GROUPS)
+    with ExitStack() as ctx:
+        const = ctx.enter_context(tc.tile_pool(name="const", bufs=1))
+        bytes_pool = ctx.enter_context(tc.tile_pool(name="bytes_pool", bufs=LOADS))
+        xb_pool = ctx.enter_context(tc.tile_pool(name="xb_pool", bufs=3))
+        g_pool = ctx.enter_context(tc.tile_pool(name="g_pool", bufs=3))
+        c_pool = ctx.enter_context(tc.tile_pool(name="c_pool", bufs=3))
+        st_pool = ctx.enter_context(tc.tile_pool(name="st_pool", bufs=5))
+        e_pool = ctx.enter_context(tc.tile_pool(name="e_pool", bufs=8))
+        o_pool = ctx.enter_context(tc.tile_pool(name="o_pool", bufs=8))
+        tp_pool = ctx.enter_context(tc.psum_pool(name="tp_pool", bufs=4))
+        qp_pool = ctx.enter_context(tc.psum_pool(name="qp_pool", bufs=4))
+        ctx.enter_context(tc.manual_schedule())
+
+        sc4 = const.tile([P, 4 * K], F32, name="sc4")
+        s_col = const.tile([P, 4], F32, name="s_col")
+        nc.sync.dma_start(out=s_col[:], in_=Q_scale.rearrange("a b (p t) -> p (a b t)", t=4))
+        q_tiles = []
+        w_sb = const.tile([P, 2, K], BF16, name="w_sb", align_bytes=64)
+        for s in range(LOADS):
+            b, sb = divmod(s, LOADS // BATCH)
+            q_bytes_sb = bytes_pool.tile([P, 4 * K], U8, name="q_bytes_sb")
+            src = Q_bytes[b].rearrange("(s p i) k -> s p (i k)", p=P, i=4)[sb]
+            if s <= 1:
+                nc.sync.dma_start(out=q_bytes_sb[:, 0:UW], in_=src[:, 0:UW])
+                if s == 1:
+                    nc.sync.dma_start(out=w_sb[:], in_=WQ.rearrange("(r p) k -> p r k", p=P))
+                nc.sync.dma_start(out=q_bytes_sb[:, UW : 2 * UW], in_=src[:, UW : 2 * UW])
+            else:
+                nc.sync.dma_start(out=q_bytes_sb[:], in_=src)
+            q_tiles.append(q_bytes_sb)
+
+        zero = const.tile([P, 1], F32, name="zero")
+        warm = const.tile([P, 1], F32, name="warm")
+        nc.vector.memset(zero[:], 0.0)
+        idle = const.tile([P, K], BF16, name="idle")
+        nc.vector.memset(idle[:], 0.0)
+        nc.scalar.activation(out=warm[:], in_=zero[:], func=ACT.Exp)
+        ident = const.tile([P, P], F32, name="ident")
+        make_identity(nc, ident[:])
+
+        state = {}
+        gx_raw = {}
+        for x in range(3):
+            gx_raw[EARLY[x]] = const.tile([P, 4, 2 * P], BF16, name="gx_raw%d" % x, align_bytes=64)
+            state[("g", EARLY[x])] = const.tile([P, UW], BF16, name="gx%d" % x, align_bytes=64)
+
+        def widen(g):
+            units = GROUPS[g]
+            n = len(units)
+            s, hf = divmod(units[0], 2)
+            xb = xb_pool.tile([P, 2 * UW], BF16, name="xb", align_bytes=64)
+            src = q_tiles[s][:, UW * hf : UW * (hf + n)].bitcast(FP8)
+            if g == 0:
+                for i in range(2):
+                    nc.vector.tensor_tensor(
+                        out=xb[:, K * i : K * (i + 1)],
+                        in0=src[:, K * i : K * (i + 1)],
+                        in1=sc4[:, 0:K],
+                        op=ALU.mult,
+                    )
+            else:
+                nc.vector.tensor_tensor(
+                    out=xb[:, 0 : UW * n], in0=src, in1=sc4[:, 0 : UW * n], op=ALU.mult
+                )
+            state[("xb", g)] = xb[:]
+
+        def cast(g):
+            s, hf = divmod(GROUPS[g][0], 2)
+            xb = xb_pool.tile([P, 2 * UW], BF16, name="xb", align_bytes=64)
+            nc.vector.tensor_copy(
+                out=xb[:, 0:UW], in_=q_tiles[s][:, UW * hf : UW * (hf + 1)].bitcast(FP8)
+            )
+            state[("xb", g)] = xb[:]
+
+        def plane(g, t):
+            u, e = divmod(t, 2)
+            src = state[("tp", g)][0][:].bitcast(BF16)[:, :, u, :]
+            nc.scalar.activation(
+                out=gx_raw[g][:, t, :].rearrange("p (i r) -> p i r", i=2),
+                in_=src.rearrange("p i (r e) -> p i r e", e=2)[:, :, :, e],
+                func=ACT.Copy,
+                scale=s_col[:, t : t + 1],
+            )
+
+        def weave(g, half):
+            nc.scalar.copy(
+                out=state[("g", g)][:, K * half : K * (half + 1)].rearrange("p (c t) -> p c t", t=4),
+                in_=gx_raw[g][:, :, P * half : P * (half + 1)].rearrange("p t c -> p c t"),
+            )
+
+        def turn(g):
+            n = 1 if g < 0 else len(GROUPS[g])
+            words = state[("xb", g)].bitcast(F32)
+            tps = []
+            for a in range(n):
+                if g in EARLY:
+                    tp = qp_pool.tile([P, 2, 2, P], F32, name="qp")
+                else:
+                    tp = tp_pool.tile([P, 2, 2, P], F32, name="tp")
+                for i in range(2):
+                    for u in range(2):
+                        c0 = 512 * a + 256 * i
+                        nc.tensor.transpose(tp[:, i, u, :], words[:, c0 + u : c0 + 256 : 2], ident[:])
+                tps.append(tp)
+            state[("tp", g)] = tps
+
+        def group(g):
+            tps = state[("tp", g)]
+            gt = g_pool.tile([P, 2 * UW], BF16, name="gt", align_bytes=64)
+            for a in range(len(tps)):
+                nc.scalar.copy(
+                    out=gt[:, UW * a : UW * (a + 1)]
+                    .bitcast(F32)
+                    .rearrange("p (i r u) -> p i r u", i=2, u=2),
+                    in_=tps[a][:].rearrange("p i u r -> p i r u"),
+                )
+            state[("g", g)] = gt
+
+        def quantize(g):
+            n = 1 if g < 0 else len(GROUPS[g])
+            gt = state[("g", g)]
+            pool = const if g < 0 else c_pool
+            codes = pool.tile([P, 512], U32, name="w_codes" if g < 0 else "codes", align_bytes=64)
+            scl = pool.tile([P, 512], U8, name="w_scl" if g < 0 else "scl", align_bytes=64)
+            nc.vector.quantize_mx(
+                out=codes[:, 0 : 256 * n].bitcast(FP8X4),
+                scales=scl[:, 0 : 256 * n],
+                in_=gt[:, 0 : UW * n],
+            )
+            state[("c", g)] = (codes, scl)
+
+        def multiply(g):
+            codes, scl = state[("c", g)]
+            w_codes, w_scl = state[("c", -1)]
+            qps = []
+            for a in range(len(GROUPS[g])):
+                qp = qp_pool.tile([P, 2, HEADS * DK], F32, name="qp")
+                for i in range(2):
+                    c0 = 256 * a + P * i
+                    nc.tensor.matmul_mx(
+                        out=qp[:, i, :],
+                        lhsT=codes[:, c0 : c0 + P].bitcast(FP8X4),
+                        lhsT_scale=scl[:, c0 : c0 + P],
+                        rhs=w_codes[:, 0:256].bitcast(FP8X4),
+                        rhs_scale=w_scl[:, 0:256],
+                        start=True,
+                        stop=True,
+                    )
+                qps.append(qp)
+            state[("qp", g)] = qps
+
+        def maxima(g):
+            qps = state[("qp", g)]
+            nm = st_pool.tile([P, 8], F32, name="nm")
+            for a in range(len(qps)):
+                nc.vector.tensor_reduce(
+                    out=nm[:, 4 * a : 4 * (a + 1)],
+                    in_=qps[a][:].rearrange("p i (h d) -> p (i h) d", h=HEADS),
+                    axis=AX.X,
+                    op=ALU.max,
+                    negate=True,
+                )
+            state[("nm", g)] = nm
+
+        def exps(g):
+            qps = state[("qp", g)]
+            nm = state[("nm", g)]
+            sm = st_pool.tile([P, 8], F32, name="sm")
+            es = []
+            for a in range(len(qps)):
+                e = e_pool.tile([P, HEADS, 2, DK], F32, name="e")
+                for i in range(2):
+                    for h in range(HEADS):
+                        c = 4 * a + 2 * i + h
+                        nc.scalar.activation(
+                            out=e[:, h, i, :],
+                            in_=qps[a][:, i, DK * h : DK * (h + 1)],
+                            func=ACT.Exp,
+                            bias=nm[:, c : c + 1],
+                            scale=1.0,
+                            accum_out=sm[:, c : c + 1],
+                        )
+                es.append(e)
+            state[("e", g)] = (es, sm)
+
+        def recip(g):
+            es, sm = state[("e", g)]
+            n = len(es)
+            rs = st_pool.tile([P, 8], F32, name="rs")
+            nc.vector.reciprocal(out=rs[:, 0 : 4 * n], in_=sm[:, 0 : 4 * n])
+            state[("rs", g)] = rs
+            state[("o", g)] = [
+                o_pool.tile([P, HEADS, 2, DK], F32, name="o") for a in range(n)
+            ]
+
+        def normalize(g, engine):
+            es, sm = state[("e", g)]
+            rs = state[("rs", g)]
+            o_tiles = state[("o", g)]
+            tail = g >= n_groups - TAIL_GROUPS
+            for a in range(len(es)):
+                for i in range(2):
+                    for h in range(HEADS):
+                        c = 4 * a + 2 * i + h
+                        if tail and len(es) == 1:
+                            who = "gpsimd" if c == 3 else ("vector" if c > 0 else "scalar")
+                        elif tail:
+                            who = "gpsimd" if c in POOL_SHARE[2] else ("vector" if c in TAIL_VECTOR else "scalar")
+                        else:
+                            who = "gpsimd" if c in POOL_SHARE[len(es)] else "scalar"
+                        if who != engine:
+                            continue
+                        dst = o_tiles[a][:, h, i, :]
+                        src = es[a][:, h, i, :]
+                        col = rs[:, c : c + 1]
+                        if who == "scalar":
+                            nc.scalar.activation(out=dst, in_=src, func=ACT.Copy, scale=col)
+                        elif who == "vector":
+                            nc.vector.tensor_scalar(
+                                out=dst, in0=src, scalar1=col, scalar2=None, op0=ALU.mult
+                            )
+                        else:
+                            nc.gpsimd.tensor_scalar(
+                                out=dst, in0=src, scalar1=col, scalar2=0.0, op0=ALU.mult, op1=ALU.add
+                            )
+
+        def store(g):
+            o_tiles = state[("o", g)]
+            for a in range(len(o_tiles)):
+                s, hf = divmod(GROUPS[g][a], 2)
+                b, sb = divmod(s, LOADS // BATCH)
+                dst = out[b].rearrange("h (s p i) d -> s p h (i d)", p=P, i=4)[sb]
+                nc.sync.dma_start(
+                    out=dst[:, :, 2 * DK * hf : 2 * DK * (hf + 1)],
+                    in_=o_tiles[a][:].rearrange("p h i d -> p h (i d)"),
+                )
+
+        junk = tp_pool.tile([P, K], F32, name="tp")
+        for w in range(WARM_MATMULS):
+            nc.tensor.matmul(out=junk[:], lhsT=idle[:, 0:P], rhs=idle[:], start=True, stop=True)
+        scp = tp_pool.tile([P, 4, P], F32, name="tp")
+        for t in range(4):
+            nc.tensor.transpose(scp[:, t, :], s_col[:, t : t + 1].to_broadcast([P, P]), ident[:])
+        nc.scalar.copy(
+            out=sc4[:, 0:K].rearrange("p (n t) -> p n t", t=4),
+            in_=scp[:].rearrange("p t n -> p n t"),
+        )
+        nc.scalar.copy(out=sc4[:, K : 2 * K], in_=sc4[:, 0:K])
+        cast(EARLY[0])
+        turn(EARLY[0])
+        for t in range(4):
+            plane(EARLY[0], t)
+        cast(EARLY[1])
+        turn(EARLY[1])
+        state[("xb", -1)] = w_sb[:].rearrange("p r k -> p (r k)")
+        turn(-1)
+        group(-1)
+        cast(EARLY[2])
+        turn(EARLY[2])
+
+        def ok(g):
+            return 0 <= g < n_groups
+
+        for it in range(-1, n_groups + 3):
+            if ok(it + 1) and it + 1 not in EARLY:
+                widen(it + 1)
+                turn(it + 1)
+            if ok(it - 3):
+                recip(it - 3)
+                normalize(it - 3, "gpsimd")
+                normalize(it - 3, "scalar")
+            if it in WEAVE_STEPS:
+                weave(EARLY[WEAVE_STEPS.index(it) // 2], WEAVE_STEPS.index(it) % 2)
+            if it == 0:
+                quantize(-1)
+            if ok(it):
+                quantize(it)
+                multiply(it)
+            if ok(it + 1) and it + 1 not in EARLY:
+                group(it + 1)
+            if it == 0:
+                nc.scalar.copy(out=sc4[:, 2 * K : 4 * K], in_=sc4[:, 0 : 2 * K])
+            if it in (-1, 0):
+                plane(EARLY[1], 2 * it + 2)
+                plane(EARLY[1], 2 * it + 3)
+            if ok(it - 1):
+                maxima(it - 1)
+                exps(it - 1)
+            if it == 1:
+                for t in range(4):
+                    plane(EARLY[2], t)
+            if ok(it - 3):
+                normalize(it - 3, "vector")
+                store(it - 3)

@@ -24,16 +24,13 @@ LOADS = 16
 UNITS = 32
 UW = 2 * K
 
-GROUPS = (
-    [[u] for u in range(3, 6)]
-    + [[u, u + 1] for u in range(6, UNITS - 2, 2)]
-    + [[UNITS - 2], [UNITS - 1], [0], [1], [2]]
-)
-EARLY = (len(GROUPS) - 3, len(GROUPS) - 2, len(GROUPS) - 1)
-WEAVE_STEPS = (4, 5, 6, 7, 8, 9)
-POOL_SHARE = {1: (3,), 2: (0, 3, 6)}
-TAIL_GROUPS = 7
-TAIL_VECTOR = (1, 2, 4, 5, 7)
+GROUPS = [[u] for u in range(0, 4)] + [[u, u + 1] for u in range(4, UNITS - 2, 2)] + [[UNITS - 2], [UNITS - 1]]
+PLANE_GROUPS = tuple(range(4, 17))
+PAIR_SHARE = "gggg"
+PLANE_SHARE = "ggggsggg"
+TAIL_GROUPS = 4
+TAIL_SHARE = {1: "svvg", 2: "gsvgsvgv"}
+VECTOR_CASTS = (0,)
 WARM_MATMULS = 4
 
 
@@ -47,13 +44,13 @@ def tile_multiheadattention_pb_t_kernel(tc, Q_bytes, Q_scale, WQ, out):
         g_pool = ctx.enter_context(tc.tile_pool(name="g_pool", bufs=3))
         c_pool = ctx.enter_context(tc.tile_pool(name="c_pool", bufs=3))
         st_pool = ctx.enter_context(tc.tile_pool(name="st_pool", bufs=5))
-        e_pool = ctx.enter_context(tc.tile_pool(name="e_pool", bufs=8))
+        e_pool = ctx.enter_context(tc.tile_pool(name="e_pool", bufs=10))
+        raw_pool = ctx.enter_context(tc.tile_pool(name="raw_pool", bufs=2))
         o_pool = ctx.enter_context(tc.tile_pool(name="o_pool", bufs=8))
         tp_pool = ctx.enter_context(tc.psum_pool(name="tp_pool", bufs=4))
         qp_pool = ctx.enter_context(tc.psum_pool(name="qp_pool", bufs=4))
         ctx.enter_context(tc.manual_schedule())
 
-        sc4 = const.tile([P, 4 * K], F32, name="sc4")
         s_col = const.tile([P, 4], F32, name="s_col")
         nc.sync.dma_start(out=s_col[:], in_=Q_scale.rearrange("a b (p t) -> p (a b t)", t=4))
         q_tiles = []
@@ -62,11 +59,10 @@ def tile_multiheadattention_pb_t_kernel(tc, Q_bytes, Q_scale, WQ, out):
             b, sb = divmod(s, LOADS // BATCH)
             q_bytes_sb = bytes_pool.tile([P, 4 * K], U8, name="q_bytes_sb")
             src = Q_bytes[b].rearrange("(s p i) k -> s p (i k)", p=P, i=4)[sb]
-            if s <= 1:
+            if s == 0:
                 nc.sync.dma_start(out=q_bytes_sb[:, 0:UW], in_=src[:, 0:UW])
-                if s == 1:
-                    nc.sync.dma_start(out=w_sb[:], in_=WQ.rearrange("(r p) k -> p r k", p=P))
                 nc.sync.dma_start(out=q_bytes_sb[:, UW : 2 * UW], in_=src[:, UW : 2 * UW])
+                nc.sync.dma_start(out=w_sb[:], in_=WQ.rearrange("(r p) k -> p r k", p=P))
             else:
                 nc.sync.dma_start(out=q_bytes_sb[:], in_=src)
             q_tiles.append(q_bytes_sb)
@@ -81,82 +77,78 @@ def tile_multiheadattention_pb_t_kernel(tc, Q_bytes, Q_scale, WQ, out):
         make_identity(nc, ident[:])
 
         state = {}
-        gx_raw = {}
-        for x in range(3):
-            gx_raw[EARLY[x]] = const.tile([P, 4, 2 * P], BF16, name="gx_raw%d" % x, align_bytes=64)
-            state[("g", EARLY[x])] = const.tile([P, UW], BF16, name="gx%d" % x, align_bytes=64)
 
-        def widen(g):
+        def cast(g):
             units = GROUPS[g]
             n = len(units)
             s, hf = divmod(units[0], 2)
             xb = xb_pool.tile([P, 2 * UW], BF16, name="xb", align_bytes=64)
             src = q_tiles[s][:, UW * hf : UW * (hf + n)].bitcast(FP8)
-            if g == 0:
-                for i in range(2):
-                    nc.vector.tensor_tensor(
-                        out=xb[:, K * i : K * (i + 1)],
-                        in0=src[:, K * i : K * (i + 1)],
-                        in1=sc4[:, 0:K],
-                        op=ALU.mult,
-                    )
+            if g in VECTOR_CASTS:
+                nc.vector.tensor_copy(out=xb[:, 0 : UW * n], in_=src)
             else:
-                nc.vector.tensor_tensor(
-                    out=xb[:, 0 : UW * n], in0=src, in1=sc4[:, 0 : UW * n], op=ALU.mult
-                )
+                nc.scalar.copy(out=xb[:, 0 : UW * n], in_=src)
             state[("xb", g)] = xb[:]
-
-        def cast(g):
-            s, hf = divmod(GROUPS[g][0], 2)
-            xb = xb_pool.tile([P, 2 * UW], BF16, name="xb", align_bytes=64)
-            nc.vector.tensor_copy(
-                out=xb[:, 0:UW], in_=q_tiles[s][:, UW * hf : UW * (hf + 1)].bitcast(FP8)
-            )
-            state[("xb", g)] = xb[:]
-
-        def plane(g, t):
-            u, e = divmod(t, 2)
-            src = state[("tp", g)][0][:].bitcast(BF16)[:, :, u, :]
-            nc.scalar.activation(
-                out=gx_raw[g][:, t, :].rearrange("p (i r) -> p i r", i=2),
-                in_=src.rearrange("p i (r e) -> p i r e", e=2)[:, :, :, e],
-                func=ACT.Copy,
-                scale=s_col[:, t : t + 1],
-            )
-
-        def weave(g, half):
-            nc.scalar.copy(
-                out=state[("g", g)][:, K * half : K * (half + 1)].rearrange("p (c t) -> p c t", t=4),
-                in_=gx_raw[g][:, :, P * half : P * (half + 1)].rearrange("p t c -> p c t"),
-            )
 
         def turn(g):
             n = 1 if g < 0 else len(GROUPS[g])
             words = state[("xb", g)].bitcast(F32)
             tps = []
             for a in range(n):
-                if g in EARLY:
-                    tp = qp_pool.tile([P, 2, 2, P], F32, name="qp")
-                else:
-                    tp = tp_pool.tile([P, 2, 2, P], F32, name="tp")
+                tp = tp_pool.tile([P, 2, 2, P], F32, name="tp")
                 for i in range(2):
                     for u in range(2):
                         c0 = 512 * a + 256 * i
-                        nc.tensor.transpose(tp[:, i, u, :], words[:, c0 + u : c0 + 256 : 2], ident[:])
+                        nc.tensor.transpose(tp[:, u, i, :], words[:, c0 + u : c0 + 256 : 2], ident[:])
                 tps.append(tp)
             state[("tp", g)] = tps
 
-        def group(g):
+        def group_weights():
+            tp = state[("tp", -1)][0]
+            gt = const.tile([P, UW], BF16, name="w_gt", align_bytes=64)
+            nc.scalar.copy(
+                out=gt[:].bitcast(F32).rearrange("p (n u) -> p n u", u=2),
+                in_=tp[:].rearrange("p u i r -> p (i r) u"),
+            )
+            state[("g", -1)] = gt
+
+        def scale(g):
             tps = state[("tp", g)]
-            gt = g_pool.tile([P, 2 * UW], BF16, name="gt", align_bytes=64)
+            gt = state[("g", g)]
             for a in range(len(tps)):
-                nc.scalar.copy(
-                    out=gt[:, UW * a : UW * (a + 1)]
-                    .bitcast(F32)
-                    .rearrange("p (i r u) -> p i r u", i=2, u=2),
-                    in_=tps[a][:].rearrange("p i u r -> p i r u"),
+                n = P if g in PLANE_GROUPS and a == 1 else 2 * P
+                src = tps[a][:].rearrange("p u i r -> p u (i r)").bitcast(BF16)
+                nc.vector.tensor_tensor(
+                    out=gt[:, UW * a : UW * a + 4 * n].rearrange("p (n u e) -> p n u e", u=2, e=2),
+                    in0=src.rearrange("p u (n e) -> p n u e", e=2)[:, 0:n],
+                    in1=s_col[:].rearrange("p (u e) -> p u e", u=2).unsqueeze(1).to_broadcast([P, n, 2, 2]),
+                    op=ALU.mult,
                 )
-            state[("g", g)] = gt
+
+        def planes(g):
+            src = state[("tp", g)][1][:].rearrange("p u i r -> p u (i r)").bitcast(BF16)
+            src = src.rearrange("p u (n e) -> p u n e", e=2)
+            raw = raw_pool.tile([P, 4, P], BF16, name="raw", align_bytes=64)
+            for t in range(4):
+                nc.scalar.activation(
+                    out=raw[:, t, :],
+                    in_=src[:, t // 2, P : 2 * P, t % 2],
+                    func=ACT.Copy,
+                    scale=s_col[:, t : t + 1],
+                )
+            state[("raw", g)] = raw
+
+        def weave(g):
+            gt = state[("g", g)]
+            raw = state[("raw", g)]
+            nc.gpsimd.tensor_scalar(
+                out=gt[:, UW + K : 2 * UW].rearrange("p (n t) -> p n t", t=4),
+                in0=raw[:].rearrange("p t n -> p n t"),
+                scalar1=1.0, scalar2=0.0, op0=ALU.mult, op1=ALU.add,
+            )
+
+        def gather(g):
+            state[("g", g)] = g_pool.tile([P, 2 * UW], BF16, name="gt", align_bytes=64)
 
         def quantize(g):
             n = 1 if g < 0 else len(GROUPS[g])
@@ -244,20 +236,15 @@ def tile_multiheadattention_pb_t_kernel(tc, Q_bytes, Q_scale, WQ, out):
                 for i in range(2):
                     for h in range(HEADS):
                         c = 4 * a + 2 * i + h
-                        if tail and len(es) == 1:
-                            who = "gpsimd" if c == 3 else ("vector" if c > 0 else "scalar")
-                        elif tail:
-                            who = "gpsimd" if c in POOL_SHARE[2] else ("vector" if c in TAIL_VECTOR else "scalar")
-                        else:
-                            who = "gpsimd" if c in POOL_SHARE[len(es)] else "scalar"
+                        who = TAIL_SHARE[len(es)][c] if tail else (PLANE_SHARE if g in PLANE_GROUPS else PAIR_SHARE)[c]
                         if who != engine:
                             continue
                         dst = o_tiles[a][:, h, i, :]
                         src = es[a][:, h, i, :]
                         col = rs[:, c : c + 1]
-                        if who == "scalar":
+                        if who == "s":
                             nc.scalar.activation(out=dst, in_=src, func=ACT.Copy, scale=col)
-                        elif who == "vector":
+                        elif who == "v":
                             nc.vector.tensor_scalar(
                                 out=dst, in0=src, scalar1=col, scalar2=None, op0=ALU.mult
                             )
@@ -280,57 +267,43 @@ def tile_multiheadattention_pb_t_kernel(tc, Q_bytes, Q_scale, WQ, out):
         junk = tp_pool.tile([P, K], F32, name="tp")
         for w in range(WARM_MATMULS):
             nc.tensor.matmul(out=junk[:], lhsT=idle[:, 0:P], rhs=idle[:], start=True, stop=True)
-        scp = tp_pool.tile([P, 4, P], F32, name="tp")
-        for t in range(4):
-            nc.tensor.transpose(scp[:, t, :], s_col[:, t : t + 1].to_broadcast([P, P]), ident[:])
-        nc.scalar.copy(
-            out=sc4[:, 0:K].rearrange("p (n t) -> p n t", t=4),
-            in_=scp[:].rearrange("p t n -> p n t"),
-        )
-        nc.scalar.copy(out=sc4[:, K : 2 * K], in_=sc4[:, 0:K])
-        cast(EARLY[0])
-        turn(EARLY[0])
-        for t in range(4):
-            plane(EARLY[0], t)
-        cast(EARLY[1])
-        turn(EARLY[1])
+        cast(0)
+        turn(0)
+        cast(1)
+        turn(1)
         state[("xb", -1)] = w_sb[:].rearrange("p r k -> p (r k)")
         turn(-1)
-        group(-1)
-        cast(EARLY[2])
-        turn(EARLY[2])
+        group_weights()
+        gather(0)
+        scale(0)
+        quantize(-1)
 
         def ok(g):
             return 0 <= g < n_groups
 
-        for it in range(-1, n_groups + 3):
-            if ok(it + 1) and it + 1 not in EARLY:
-                widen(it + 1)
-                turn(it + 1)
-            if ok(it - 3):
-                recip(it - 3)
-                normalize(it - 3, "gpsimd")
-                normalize(it - 3, "scalar")
-            if it in WEAVE_STEPS:
-                weave(EARLY[WEAVE_STEPS.index(it) // 2], WEAVE_STEPS.index(it) % 2)
-            if it == 0:
-                quantize(-1)
+        for it in range(0, n_groups + 3):
+            if ok(it + 1):
+                gather(it + 1)
+                if it + 1 in PLANE_GROUPS:
+                    planes(it + 1)
+                    weave(it + 1)
+            if ok(it + 2):
+                cast(it + 2)
             if ok(it):
                 quantize(it)
                 multiply(it)
-            if ok(it + 1) and it + 1 not in EARLY:
-                group(it + 1)
-            if it == 0:
-                nc.scalar.copy(out=sc4[:, 2 * K : 4 * K], in_=sc4[:, 0 : 2 * K])
-            if it in (-1, 0):
-                plane(EARLY[1], 2 * it + 2)
-                plane(EARLY[1], 2 * it + 3)
+            if ok(it + 2):
+                turn(it + 2)
+            if ok(it - 2):
+                recip(it - 2)
+                normalize(it - 2, "g")
+                normalize(it - 2, "s")
+                normalize(it - 2, "v")
             if ok(it - 1):
-                maxima(it - 1)
                 exps(it - 1)
-            if it == 1:
-                for t in range(4):
-                    plane(EARLY[2], t)
-            if ok(it - 3):
-                normalize(it - 3, "vector")
-                store(it - 3)
+            if ok(it + 1):
+                scale(it + 1)
+            if ok(it):
+                maxima(it)
+            if ok(it - 2):
+                store(it - 2)

@@ -25,8 +25,8 @@ UNITS = 32
 UW = 2 * K
 
 GROUPS = [[u] for u in range(0, 4)] + [[u, u + 1] for u in range(4, UNITS - 2, 2)] + [[UNITS - 2], [UNITS - 1]]
-PLANE_GROUPS = tuple(range(4, 17))
-PAIR_SHARE = "gggg"
+PLANE_GROUPS = ()
+PAIR_SHARE = "gggggggg"
 PLANE_SHARE = "ggggsggg"
 TAIL_GROUPS = 4
 TAIL_SHARE = {1: "svvg", 2: "gsvgsvgv"}

@@ -25,13 +25,15 @@ UNITS = 32
 UW = 2 * K
 
 GROUPS = [[u] for u in range(0, 4)] + [[u, u + 1] for u in range(4, UNITS - 2, 2)] + [[UNITS - 2], [UNITS - 1]]
-PLANE_GROUPS = ()
+PLANE_GROUPS = tuple(range(4, 17))
 PAIR_SHARE = "gggggggg"
-PLANE_SHARE = "ggggsggg"
+PLANE_SHARE = "gsgsgsgs"
 TAIL_GROUPS = 4
 TAIL_SHARE = {1: "svvg", 2: "gsvgsvgv"}
-VECTOR_CASTS = (0,)
+GN = 128
 WARM_MATMULS = 4
+LAG = 2
+FRONT = 1
 
 
 def tile_multiheadattention_pb_t_kernel(tc, Q_bytes, Q_scale, WQ, out):
@@ -45,7 +47,7 @@ def tile_multiheadattention_pb_t_kernel(tc, Q_bytes, Q_scale, WQ, out):
         c_pool = ctx.enter_context(tc.tile_pool(name="c_pool", bufs=3))
         st_pool = ctx.enter_context(tc.tile_pool(name="st_pool", bufs=5))
         e_pool = ctx.enter_context(tc.tile_pool(name="e_pool", bufs=10))
-        raw_pool = ctx.enter_context(tc.tile_pool(name="raw_pool", bufs=2))
+        raw_pool = ctx.enter_context(tc.tile_pool(name="raw_pool", bufs=3))
         o_pool = ctx.enter_context(tc.tile_pool(name="o_pool", bufs=8))
         tp_pool = ctx.enter_context(tc.psum_pool(name="tp_pool", bufs=4))
         qp_pool = ctx.enter_context(tc.psum_pool(name="qp_pool", bufs=4))
@@ -78,13 +80,13 @@ def tile_multiheadattention_pb_t_kernel(tc, Q_bytes, Q_scale, WQ, out):
 
         state = {}
 
-        def cast(g):
+        def cast(g, engine):
             units = GROUPS[g]
             n = len(units)
             s, hf = divmod(units[0], 2)
             xb = xb_pool.tile([P, 2 * UW], BF16, name="xb", align_bytes=64)
             src = q_tiles[s][:, UW * hf : UW * (hf + n)].bitcast(FP8)
-            if g in VECTOR_CASTS:
+            if engine == "v":
                 nc.vector.tensor_copy(out=xb[:, 0 : UW * n], in_=src)
             else:
                 nc.scalar.copy(out=xb[:, 0 : UW * n], in_=src)
@@ -116,7 +118,7 @@ def tile_multiheadattention_pb_t_kernel(tc, Q_bytes, Q_scale, WQ, out):
             tps = state[("tp", g)]
             gt = state[("g", g)]
             for a in range(len(tps)):
-                n = P if g in PLANE_GROUPS and a == 1 else 2 * P
+                n = 2 * P - GN if g in PLANE_GROUPS and a == 1 else 2 * P
                 src = tps[a][:].rearrange("p u i r -> p u (i r)").bitcast(BF16)
                 nc.vector.tensor_tensor(
                     out=gt[:, UW * a : UW * a + 4 * n].rearrange("p (n u e) -> p n u e", u=2, e=2),
@@ -126,25 +128,20 @@ def tile_multiheadattention_pb_t_kernel(tc, Q_bytes, Q_scale, WQ, out):
                 )
 
         def planes(g):
-            src = state[("tp", g)][1][:].rearrange("p u i r -> p u (i r)").bitcast(BF16)
-            src = src.rearrange("p u (n e) -> p u n e", e=2)
-            raw = raw_pool.tile([P, 4, P], BF16, name="raw", align_bytes=64)
-            for t in range(4):
-                nc.scalar.activation(
-                    out=raw[:, t, :],
-                    in_=src[:, t // 2, P : 2 * P, t % 2],
-                    func=ACT.Copy,
-                    scale=s_col[:, t : t + 1],
-                )
+            raw = raw_pool.tile([P, GN, 4], BF16, name="raw", align_bytes=64)
+            nc.scalar.copy(
+                out=raw[:].rearrange("p n t -> p (n t)").bitcast(F32).rearrange("p (n u) -> p n u", u=2),
+                in_=state[("tp", g)][1][:].rearrange("p u i r -> p (i r) u")[:, 2 * P - GN : 2 * P, :],
+            )
             state[("raw", g)] = raw
 
         def weave(g):
             gt = state[("g", g)]
-            raw = state[("raw", g)]
-            nc.gpsimd.tensor_scalar(
-                out=gt[:, UW + K : 2 * UW].rearrange("p (n t) -> p n t", t=4),
-                in0=raw[:].rearrange("p t n -> p n t"),
-                scalar1=1.0, scalar2=0.0, op0=ALU.mult, op1=ALU.add,
+            nc.gpsimd.tensor_tensor(
+                out=gt[:, 2 * UW - 4 * GN : 2 * UW].rearrange("p (n t) -> p n t", t=4),
+                in0=state[("raw", g)][:],
+                in1=s_col[:].unsqueeze(1).to_broadcast([P, GN, 4]),
+                op=ALU.mult,
             )
 
         def gather(g):
@@ -227,7 +224,7 @@ def tile_multiheadattention_pb_t_kernel(tc, Q_bytes, Q_scale, WQ, out):
                 o_pool.tile([P, HEADS, 2, DK], F32, name="o") for a in range(n)
             ]
 
-        def normalize(g, engine):
+        def normalize(g, engine, lo=0, hi=8):
             es, sm = state[("e", g)]
             rs = state[("rs", g)]
             o_tiles = state[("o", g)]
@@ -237,7 +234,7 @@ def tile_multiheadattention_pb_t_kernel(tc, Q_bytes, Q_scale, WQ, out):
                     for h in range(HEADS):
                         c = 4 * a + 2 * i + h
                         who = TAIL_SHARE[len(es)][c] if tail else (PLANE_SHARE if g in PLANE_GROUPS else PAIR_SHARE)[c]
-                        if who != engine:
+                        if who != engine or not lo <= c < hi:
                             continue
                         dst = o_tiles[a][:, h, i, :]
                         src = es[a][:, h, i, :]
@@ -264,46 +261,53 @@ def tile_multiheadattention_pb_t_kernel(tc, Q_bytes, Q_scale, WQ, out):
                     in_=o_tiles[a][:].rearrange("p h i d -> p h (i d)"),
                 )
 
+        def ok(g):
+            return 0 <= g < n_groups
+
         junk = tp_pool.tile([P, K], F32, name="tp")
         for w in range(WARM_MATMULS):
             nc.tensor.matmul(out=junk[:], lhsT=idle[:, 0:P], rhs=idle[:], start=True, stop=True)
-        cast(0)
+        cast(0, "v")
         turn(0)
-        cast(1)
+        cast(1, "s")
         turn(1)
         state[("xb", -1)] = w_sb[:].rearrange("p r k -> p (r k)")
         turn(-1)
-        group_weights()
         gather(0)
         scale(0)
-        quantize(-1)
-
-        def ok(g):
-            return 0 <= g < n_groups
+        group_weights()
+        cast(2, "s")
 
         for it in range(0, n_groups + 3):
             if ok(it + 1):
                 gather(it + 1)
-                if it + 1 in PLANE_GROUPS:
-                    planes(it + 1)
-                    weave(it + 1)
-            if ok(it + 2):
-                cast(it + 2)
+            if it == 0:
+                scale(1)
+                quantize(-1)
             if ok(it):
                 quantize(it)
                 multiply(it)
             if ok(it + 2):
                 turn(it + 2)
-            if ok(it - 2):
-                recip(it - 2)
-                normalize(it - 2, "g")
-                normalize(it - 2, "s")
-                normalize(it - 2, "v")
+            if ok(it - LAG):
+                recip(it - LAG)
+                normalize(it - LAG, "g", 0, FRONT)
+            if ok(it + 1) and it + 1 in PLANE_GROUPS:
+                weave(it + 1)
+            if ok(it - LAG):
+                normalize(it - LAG, "g", FRONT, 8)
             if ok(it - 1):
                 exps(it - 1)
-            if ok(it + 1):
+            if ok(it - LAG):
+                normalize(it - LAG, "s")
+            if ok(it + 3):
+                cast(it + 3, "s")
+            if ok(it + 2) and it + 2 in PLANE_GROUPS:
+                planes(it + 2)
+            if ok(it + 1) and it > 0:
                 scale(it + 1)
             if ok(it):
                 maxima(it)
-            if ok(it - 2):
-                store(it - 2)
+            if ok(it - LAG):
+                normalize(it - LAG, "v")
+                store(it - LAG)

@@ -21,19 +21,21 @@ BATCH = 4
 HEADS = 2
 DK = 128
 LOADS = 16
-UNITS = 32
-UW = 2 * K
+BLOCKS = 64
+BW = K
 
-GROUPS = [[u] for u in range(0, 4)] + [[u, u + 1] for u in range(4, UNITS - 2, 2)] + [[UNITS - 2], [UNITS - 1]]
-PLANE_GROUPS = tuple(range(4, 17))
-PAIR_SHARE = "gggggggg"
-PLANE_SHARE = "gsgsgsgs"
-TAIL_GROUPS = 4
-TAIL_SHARE = {1: "svvg", 2: "gsvgsvgv"}
+FIRST_SIZES = [1, 1, 2]
+LAST_SIZES = [2, 1, 1]
+SIZES = FIRST_SIZES + [4] * ((BLOCKS - sum(FIRST_SIZES) - sum(LAST_SIZES)) // 4) + LAST_SIZES
+GROUPS = [(sum(SIZES[:g]), SIZES[g]) for g in range(len(SIZES))]
 GN = 128
-WARM_MATMULS = 4
 LAG = 2
 FRONT = 1
+SHARE = {1: "gg", 2: "gggg", 4: "gsgsgsgs"}
+TAIL_GROUPS = 4
+TAIL_SHARE = {1: "sv", 2: "svvg", 4: "gsvgsvgv"}
+HEAD_CASTS = "vs"
+WARM_MATMULS = 4
 
 
 def tile_multiheadattention_pb_t_kernel(tc, Q_bytes, Q_scale, WQ, out):
@@ -43,11 +45,11 @@ def tile_multiheadattention_pb_t_kernel(tc, Q_bytes, Q_scale, WQ, out):
         const = ctx.enter_context(tc.tile_pool(name="const", bufs=1))
         bytes_pool = ctx.enter_context(tc.tile_pool(name="bytes_pool", bufs=LOADS))
         xb_pool = ctx.enter_context(tc.tile_pool(name="xb_pool", bufs=3))
+        raw_pool = ctx.enter_context(tc.tile_pool(name="raw_pool", bufs=3))
         g_pool = ctx.enter_context(tc.tile_pool(name="g_pool", bufs=3))
         c_pool = ctx.enter_context(tc.tile_pool(name="c_pool", bufs=3))
         st_pool = ctx.enter_context(tc.tile_pool(name="st_pool", bufs=5))
         e_pool = ctx.enter_context(tc.tile_pool(name="e_pool", bufs=10))
-        raw_pool = ctx.enter_context(tc.tile_pool(name="raw_pool", bufs=3))
         o_pool = ctx.enter_context(tc.tile_pool(name="o_pool", bufs=8))
         tp_pool = ctx.enter_context(tc.psum_pool(name="tp_pool", bufs=4))
         qp_pool = ctx.enter_context(tc.psum_pool(name="qp_pool", bufs=4))
@@ -62,8 +64,8 @@ def tile_multiheadattention_pb_t_kernel(tc, Q_bytes, Q_scale, WQ, out):
             q_bytes_sb = bytes_pool.tile([P, 4 * K], U8, name="q_bytes_sb")
             src = Q_bytes[b].rearrange("(s p i) k -> s p (i k)", p=P, i=4)[sb]
             if s == 0:
-                nc.sync.dma_start(out=q_bytes_sb[:, 0:UW], in_=src[:, 0:UW])
-                nc.sync.dma_start(out=q_bytes_sb[:, UW : 2 * UW], in_=src[:, UW : 2 * UW])
+                nc.sync.dma_start(out=q_bytes_sb[:, 0 : 2 * K], in_=src[:, 0 : 2 * K])
+                nc.sync.dma_start(out=q_bytes_sb[:, 2 * K : 4 * K], in_=src[:, 2 * K : 4 * K])
                 nc.sync.dma_start(out=w_sb[:], in_=WQ.rearrange("(r p) k -> p r k", p=P))
             else:
                 nc.sync.dma_start(out=q_bytes_sb[:], in_=src)
@@ -80,54 +82,63 @@ def tile_multiheadattention_pb_t_kernel(tc, Q_bytes, Q_scale, WQ, out):
 
         state = {}
 
+        def ok(g):
+            return 0 <= g < n_groups
+
+        def big(g):
+            return ok(g) and GROUPS[g][1] == 4
+
+        def banks(n):
+            return [(a, min(2, n - a)) for a in range(0, n, 2)]
+
         def cast(g, engine):
-            units = GROUPS[g]
-            n = len(units)
-            s, hf = divmod(units[0], 2)
-            xb = xb_pool.tile([P, 2 * UW], BF16, name="xb", align_bytes=64)
-            src = q_tiles[s][:, UW * hf : UW * (hf + n)].bitcast(FP8)
+            first, n = GROUPS[g]
+            s, i = divmod(first, 4)
+            xb = xb_pool.tile([P, 4 * BW], BF16, name="xb", align_bytes=64)
+            src = q_tiles[s][:, BW * i : BW * (i + n)].bitcast(FP8)
             if engine == "v":
-                nc.vector.tensor_copy(out=xb[:, 0 : UW * n], in_=src)
+                nc.vector.tensor_copy(out=xb[:, 0 : BW * n], in_=src)
             else:
-                nc.scalar.copy(out=xb[:, 0 : UW * n], in_=src)
+                nc.scalar.copy(out=xb[:, 0 : BW * n], in_=src)
             state[("xb", g)] = xb[:]
 
         def turn(g):
-            n = 1 if g < 0 else len(GROUPS[g])
+            n = 2 if g < 0 else GROUPS[g][1]
             words = state[("xb", g)].bitcast(F32)
             tps = []
-            for a in range(n):
+            for a, m in banks(n):
                 tp = tp_pool.tile([P, 2, 2, P], F32, name="tp")
-                for i in range(2):
+                for i in range(m):
                     for u in range(2):
-                        c0 = 512 * a + 256 * i
+                        c0 = 256 * (a + i)
                         nc.tensor.transpose(tp[:, u, i, :], words[:, c0 + u : c0 + 256 : 2], ident[:])
                 tps.append(tp)
             state[("tp", g)] = tps
 
         def group_weights():
-            tp = state[("tp", -1)][0]
-            gt = const.tile([P, UW], BF16, name="w_gt", align_bytes=64)
+            gt = const.tile([P, 2 * BW], BF16, name="w_gt", align_bytes=64)
             nc.scalar.copy(
                 out=gt[:].bitcast(F32).rearrange("p (n u) -> p n u", u=2),
-                in_=tp[:].rearrange("p u i r -> p (i r) u"),
+                in_=state[("tp", -1)][0][:].rearrange("p u i r -> p (i r) u"),
             )
             state[("g", -1)] = gt
 
+        def gather(g):
+            state[("g", g)] = g_pool.tile([P, 4 * BW], BF16, name="gt", align_bytes=64)
+
         def scale(g):
-            tps = state[("tp", g)]
             gt = state[("g", g)]
-            for a in range(len(tps)):
-                n = 2 * P - GN if g in PLANE_GROUPS and a == 1 else 2 * P
-                src = tps[a][:].rearrange("p u i r -> p u (i r)").bitcast(BF16)
+            for (a, m), tp in zip(banks(GROUPS[g][1]), state[("tp", g)]):
+                n = P * m - (GN if big(g) and a == 2 else 0)
+                src = tp[:].rearrange("p u i r -> p u (i r)").bitcast(BF16)
                 nc.vector.tensor_tensor(
-                    out=gt[:, UW * a : UW * a + 4 * n].rearrange("p (n u e) -> p n u e", u=2, e=2),
+                    out=gt[:, BW * a : BW * a + 4 * n].rearrange("p (n u e) -> p n u e", u=2, e=2),
                     in0=src.rearrange("p u (n e) -> p n u e", e=2)[:, 0:n],
                     in1=s_col[:].rearrange("p (u e) -> p u e", u=2).unsqueeze(1).to_broadcast([P, n, 2, 2]),
                     op=ALU.mult,
                 )
 
-        def planes(g):
+        def copy_words(g):
             raw = raw_pool.tile([P, GN, 4], BF16, name="raw", align_bytes=64)
             nc.scalar.copy(
                 out=raw[:].rearrange("p n t -> p (n t)").bitcast(F32).rearrange("p (n u) -> p n u", u=2),
@@ -135,28 +146,23 @@ def tile_multiheadattention_pb_t_kernel(tc, Q_bytes, Q_scale, WQ, out):
             )
             state[("raw", g)] = raw
 
-        def weave(g):
-            gt = state[("g", g)]
+        def scale_gpsimd(g):
             nc.gpsimd.tensor_tensor(
-                out=gt[:, 2 * UW - 4 * GN : 2 * UW].rearrange("p (n t) -> p n t", t=4),
+                out=state[("g", g)][:, 4 * (BW - GN) : 4 * BW].rearrange("p (n t) -> p n t", t=4),
                 in0=state[("raw", g)][:],
                 in1=s_col[:].unsqueeze(1).to_broadcast([P, GN, 4]),
                 op=ALU.mult,
             )
 
-        def gather(g):
-            state[("g", g)] = g_pool.tile([P, 2 * UW], BF16, name="gt", align_bytes=64)
-
         def quantize(g):
-            n = 1 if g < 0 else len(GROUPS[g])
-            gt = state[("g", g)]
+            n = 2 if g < 0 else GROUPS[g][1]
             pool = const if g < 0 else c_pool
-            codes = pool.tile([P, 512], U32, name="w_codes" if g < 0 else "codes", align_bytes=64)
-            scl = pool.tile([P, 512], U8, name="w_scl" if g < 0 else "scl", align_bytes=64)
+            codes = pool.tile([P, 4 * P], U32, name="w_codes" if g < 0 else "codes", align_bytes=64)
+            scl = pool.tile([P, 4 * P], U8, name="w_scl" if g < 0 else "scl", align_bytes=64)
             nc.vector.quantize_mx(
-                out=codes[:, 0 : 256 * n].bitcast(FP8X4),
-                scales=scl[:, 0 : 256 * n],
-                in_=gt[:, 0 : UW * n],
+                out=codes[:, 0 : P * n].bitcast(FP8X4),
+                scales=scl[:, 0 : P * n],
+                in_=state[("g", g)][:, 0 : BW * n],
             )
             state[("c", g)] = (codes, scl)
 
@@ -164,10 +170,10 @@ def tile_multiheadattention_pb_t_kernel(tc, Q_bytes, Q_scale, WQ, out):
             codes, scl = state[("c", g)]
             w_codes, w_scl = state[("c", -1)]
             qps = []
-            for a in range(len(GROUPS[g])):
+            for a, m in banks(GROUPS[g][1]):
                 qp = qp_pool.tile([P, 2, HEADS * DK], F32, name="qp")
-                for i in range(2):
-                    c0 = 256 * a + P * i
+                for i in range(m):
+                    c0 = P * (a + i)
                     nc.tensor.matmul_mx(
                         out=qp[:, i, :],
                         lhsT=codes[:, c0 : c0 + P].bitcast(FP8X4),
@@ -181,95 +187,87 @@ def tile_multiheadattention_pb_t_kernel(tc, Q_bytes, Q_scale, WQ, out):
             state[("qp", g)] = qps
 
         def maxima(g):
-            qps = state[("qp", g)]
             nm = st_pool.tile([P, 8], F32, name="nm")
-            for a in range(len(qps)):
+            for (a, m), qp in zip(banks(GROUPS[g][1]), state[("qp", g)]):
                 nc.vector.tensor_reduce(
-                    out=nm[:, 4 * a : 4 * (a + 1)],
-                    in_=qps[a][:].rearrange("p i (h d) -> p (i h) d", h=HEADS),
+                    out=nm[:, 2 * a : 2 * (a + m)],
+                    in_=qp[:, 0:m, :].rearrange("p i (h d) -> p (i h) d", h=HEADS),
                     axis=AX.X,
                     op=ALU.max,
                     negate=True,
                 )
             state[("nm", g)] = nm
 
+        def panels(g):
+            return [(a, i, h) for a, m in banks(GROUPS[g][1]) for i in range(m) for h in range(HEADS)]
+
         def exps(g):
             qps = state[("qp", g)]
             nm = state[("nm", g)]
             sm = st_pool.tile([P, 8], F32, name="sm")
             es = []
-            for a in range(len(qps)):
+            for a, m in banks(GROUPS[g][1]):
                 e = e_pool.tile([P, HEADS, 2, DK], F32, name="e")
-                for i in range(2):
-                    for h in range(HEADS):
-                        c = 4 * a + 2 * i + h
-                        nc.scalar.activation(
-                            out=e[:, h, i, :],
-                            in_=qps[a][:, i, DK * h : DK * (h + 1)],
-                            func=ACT.Exp,
-                            bias=nm[:, c : c + 1],
-                            scale=1.0,
-                            accum_out=sm[:, c : c + 1],
-                        )
                 es.append(e)
+            for c, (a, i, h) in enumerate(panels(g)):
+                nc.scalar.activation(
+                    out=es[a // 2][:, h, i, :],
+                    in_=qps[a // 2][:, i, DK * h : DK * (h + 1)],
+                    func=ACT.Exp,
+                    bias=nm[:, c : c + 1],
+                    scale=1.0,
+                    accum_out=sm[:, c : c + 1],
+                )
             state[("e", g)] = (es, sm)
 
         def recip(g):
             es, sm = state[("e", g)]
-            n = len(es)
+            n = 2 * GROUPS[g][1]
             rs = st_pool.tile([P, 8], F32, name="rs")
-            nc.vector.reciprocal(out=rs[:, 0 : 4 * n], in_=sm[:, 0 : 4 * n])
+            nc.vector.reciprocal(out=rs[:, 0:n], in_=sm[:, 0:n])
             state[("rs", g)] = rs
-            state[("o", g)] = [
-                o_pool.tile([P, HEADS, 2, DK], F32, name="o") for a in range(n)
-            ]
+            os_ = []
+            for a, m in banks(GROUPS[g][1]):
+                o = o_pool.tile([P, HEADS, 2, DK], F32, name="o")
+                os_.append(o)
+            state[("o", g)] = os_
 
         def normalize(g, engine, lo=0, hi=8):
             es, sm = state[("e", g)]
             rs = state[("rs", g)]
-            o_tiles = state[("o", g)]
-            tail = g >= n_groups - TAIL_GROUPS
-            for a in range(len(es)):
-                for i in range(2):
-                    for h in range(HEADS):
-                        c = 4 * a + 2 * i + h
-                        who = TAIL_SHARE[len(es)][c] if tail else (PLANE_SHARE if g in PLANE_GROUPS else PAIR_SHARE)[c]
-                        if who != engine or not lo <= c < hi:
-                            continue
-                        dst = o_tiles[a][:, h, i, :]
-                        src = es[a][:, h, i, :]
-                        col = rs[:, c : c + 1]
-                        if who == "s":
-                            nc.scalar.activation(out=dst, in_=src, func=ACT.Copy, scale=col)
-                        elif who == "v":
-                            nc.vector.tensor_scalar(
-                                out=dst, in0=src, scalar1=col, scalar2=None, op0=ALU.mult
-                            )
-                        else:
-                            nc.gpsimd.tensor_scalar(
-                                out=dst, in0=src, scalar1=col, scalar2=0.0, op0=ALU.mult, op1=ALU.add
-                            )
+            share = (TAIL_SHARE if g >= n_groups - TAIL_GROUPS else SHARE)[GROUPS[g][1]]
+            for c, (a, i, h) in enumerate(panels(g)):
+                if share[c] != engine or not lo <= c < hi:
+                    continue
+                dst = state[("o", g)][a // 2][:, h, i, :]
+                src = es[a // 2][:, h, i, :]
+                col = rs[:, c : c + 1]
+                if engine == "s":
+                    nc.scalar.activation(out=dst, in_=src, func=ACT.Copy, scale=col)
+                elif engine == "v":
+                    nc.vector.tensor_scalar(out=dst, in0=src, scalar1=col, scalar2=None, op0=ALU.mult)
+                else:
+                    nc.gpsimd.tensor_scalar(
+                        out=dst, in0=src, scalar1=col, scalar2=0.0, op0=ALU.mult, op1=ALU.add
+                    )
 
         def store(g):
-            o_tiles = state[("o", g)]
-            for a in range(len(o_tiles)):
-                s, hf = divmod(GROUPS[g][a], 2)
+            first, n = GROUPS[g]
+            for (a, m), o in zip(banks(n), state[("o", g)]):
+                s, i = divmod(first + a, 4)
                 b, sb = divmod(s, LOADS // BATCH)
                 dst = out[b].rearrange("h (s p i) d -> s p h (i d)", p=P, i=4)[sb]
                 nc.sync.dma_start(
-                    out=dst[:, :, 2 * DK * hf : 2 * DK * (hf + 1)],
-                    in_=o_tiles[a][:].rearrange("p h i d -> p h (i d)"),
+                    out=dst[:, :, DK * i : DK * (i + m)],
+                    in_=o[:, :, 0:m, :].rearrange("p h i d -> p h (i d)"),
                 )
-
-        def ok(g):
-            return 0 <= g < n_groups
 
         junk = tp_pool.tile([P, K], F32, name="tp")
         for w in range(WARM_MATMULS):
             nc.tensor.matmul(out=junk[:], lhsT=idle[:, 0:P], rhs=idle[:], start=True, stop=True)
-        cast(0, "v")
+        cast(0, HEAD_CASTS[0])
         turn(0)
-        cast(1, "s")
+        cast(1, HEAD_CASTS[1])
         turn(1)
         state[("xb", -1)] = w_sb[:].rearrange("p r k -> p (r k)")
         turn(-1)
@@ -278,7 +276,7 @@ def tile_multiheadattention_pb_t_kernel(tc, Q_bytes, Q_scale, WQ, out):
         group_weights()
         cast(2, "s")
 
-        for it in range(0, n_groups + 3):
+        for it in range(0, n_groups + LAG):
             if ok(it + 1):
                 gather(it + 1)
             if it == 0:
@@ -292,8 +290,8 @@ def tile_multiheadattention_pb_t_kernel(tc, Q_bytes, Q_scale, WQ, out):
             if ok(it - LAG):
                 recip(it - LAG)
                 normalize(it - LAG, "g", 0, FRONT)
-            if ok(it + 1) and it + 1 in PLANE_GROUPS:
-                weave(it + 1)
+            if big(it + 1):
+                scale_gpsimd(it + 1)
             if ok(it - LAG):
                 normalize(it - LAG, "g", FRONT, 8)
             if ok(it - 1):
@@ -302,8 +300,8 @@ def tile_multiheadattention_pb_t_kernel(tc, Q_bytes, Q_scale, WQ, out):
                 normalize(it - LAG, "s")
             if ok(it + 3):
                 cast(it + 3, "s")
-            if ok(it + 2) and it + 2 in PLANE_GROUPS:
-                planes(it + 2)
+            if big(it + 2):
+                copy_words(it + 2)
             if ok(it + 1) and it > 0:
                 scale(it + 1)
             if ok(it):

@@ -282,13 +282,14 @@ def tile_multiheadattention_pb_t_kernel(tc, Q_bytes, Q_scale, WQ, out):
             if it == 0:
                 scale(1)
                 quantize(-1)
+            if ok(it - LAG):
+                recip(it - LAG)
             if ok(it):
                 quantize(it)
                 multiply(it)
             if ok(it + 2):
                 turn(it + 2)
             if ok(it - LAG):
-                recip(it - LAG)
                 normalize(it - LAG, "g", 0, FRONT)
             if big(it + 1):
                 scale_gpsimd(it + 1)

@@ -31,9 +31,9 @@ GROUPS = [(sum(SIZES[:g]), SIZES[g]) for g in range(len(SIZES))]
 GN = 128
 LAG = 2
 FRONT = 1
-SHARE = {1: "gg", 2: "gggg", 4: "gsgsgsgs"}
-TAIL_GROUPS = 4
-TAIL_SHARE = {1: "sv", 2: "svvg", 4: "gsvgsvgv"}
+SHARE = {1: "gg", 2: "gggg", 4: "gsgsgsss"}
+TAIL_GROUPS = 3
+TAIL_SHARE = {1: "sv", 2: "svvg", 4: "gsgsgsgs"}
 HEAD_CASTS = "vs"
 WARM_MATMULS = 4
 
@@ -56,7 +56,6 @@ def tile_multiheadattention_pb_t_kernel(tc, Q_bytes, Q_scale, WQ, out):
         ctx.enter_context(tc.manual_schedule())
 
         s_col = const.tile([P, 4], F32, name="s_col")
-        nc.sync.dma_start(out=s_col[:], in_=Q_scale.rearrange("a b (p t) -> p (a b t)", t=4))
         q_tiles = []
         w_sb = const.tile([P, 2, K], BF16, name="w_sb", align_bytes=64)
         for s in range(LOADS):
@@ -64,7 +63,9 @@ def tile_multiheadattention_pb_t_kernel(tc, Q_bytes, Q_scale, WQ, out):
             q_bytes_sb = bytes_pool.tile([P, 4 * K], U8, name="q_bytes_sb")
             src = Q_bytes[b].rearrange("(s p i) k -> s p (i k)", p=P, i=4)[sb]
             if s == 0:
-                nc.sync.dma_start(out=q_bytes_sb[:, 0 : 2 * K], in_=src[:, 0 : 2 * K])
+                nc.sync.dma_start(out=q_bytes_sb[:, 0:K], in_=src[:, 0:K])
+                nc.sync.dma_start(out=s_col[:], in_=Q_scale.rearrange("a b (p t) -> p (a b t)", t=4))
+                nc.sync.dma_start(out=q_bytes_sb[:, K : 2 * K], in_=src[:, K : 2 * K])
                 nc.sync.dma_start(out=q_bytes_sb[:, 2 * K : 4 * K], in_=src[:, 2 * K : 4 * K])
                 nc.sync.dma_start(out=w_sb[:], in_=WQ.rearrange("(r p) k -> p r k", p=P))
             else:
@@ -276,7 +277,7 @@ def tile_multiheadattention_pb_t_kernel(tc, Q_bytes, Q_scale, WQ, out):
         group_weights()
         cast(2, "s")
 
-        for it in range(0, n_groups + LAG):
+        for it in range(0, n_groups + LAG + 1):
             if ok(it + 1):
                 gather(it + 1)
             if it == 0:
@@ -287,6 +288,9 @@ def tile_multiheadattention_pb_t_kernel(tc, Q_bytes, Q_scale, WQ, out):
             if ok(it):
                 quantize(it)
                 multiply(it)
+            if ok(it - LAG - 1):
+                normalize(it - LAG - 1, "v")
+                store(it - LAG - 1)
             if ok(it + 2):
                 turn(it + 2)
             if ok(it - LAG):
@@ -307,6 +311,3 @@ def tile_multiheadattention_pb_t_kernel(tc, Q_bytes, Q_scale, WQ, out):
                 scale(it + 1)
             if ok(it):
                 maxima(it)
-            if ok(it - LAG):
-                normalize(it - LAG, "v")
-                store(it - LAG)

@@ -28,13 +28,13 @@ FIRST_SIZES = [1, 1, 2]
 LAST_SIZES = [2, 1, 1]
 SIZES = FIRST_SIZES + [4] * ((BLOCKS - sum(FIRST_SIZES) - sum(LAST_SIZES)) // 4) + LAST_SIZES
 GROUPS = [(sum(SIZES[:g]), SIZES[g]) for g in range(len(SIZES))]
-GN = 128
+GN = 144
 LAG = 2
-FRONT = 1
-SHARE = {1: "gg", 2: "gggg", 4: "gsgsgsss"}
+LEAD = 2
+FRONT = 8
+SHARE = {1: "gg", 2: "gggg", 4: "ggggssss"}
 TAIL_GROUPS = 3
 TAIL_SHARE = {1: "sv", 2: "svvg", 4: "gsgsgsgs"}
-HEAD_CASTS = "vs"
 WARM_MATMULS = 4
 
 
@@ -46,7 +46,7 @@ def tile_multiheadattention_pb_t_kernel(tc, Q_bytes, Q_scale, WQ, out):
         bytes_pool = ctx.enter_context(tc.tile_pool(name="bytes_pool", bufs=LOADS))
         xb_pool = ctx.enter_context(tc.tile_pool(name="xb_pool", bufs=3))
         raw_pool = ctx.enter_context(tc.tile_pool(name="raw_pool", bufs=3))
-        g_pool = ctx.enter_context(tc.tile_pool(name="g_pool", bufs=3))
+        g_pool = ctx.enter_context(tc.tile_pool(name="g_pool", bufs=4))
         c_pool = ctx.enter_context(tc.tile_pool(name="c_pool", bufs=3))
         st_pool = ctx.enter_context(tc.tile_pool(name="st_pool", bufs=5))
         e_pool = ctx.enter_context(tc.tile_pool(name="e_pool", bufs=10))
@@ -240,6 +240,15 @@ def tile_multiheadattention_pb_t_kernel(tc, Q_bytes, Q_scale, WQ, out):
             for c, (a, i, h) in enumerate(panels(g)):
                 if share[c] != engine or not lo <= c < hi:
                     continue
+                if engine == "g" and len(share) == 8:
+                    if c % 4 == 0:
+                        nc.gpsimd.tensor_tensor(
+                            out=state[("o", g)][a // 2][:],
+                            in0=es[a // 2][:],
+                            in1=rs[:, c : c + 4].rearrange("p (i h) -> p h i", h=HEADS).unsqueeze(3).to_broadcast([P, HEADS, 2, DK]),
+                            op=ALU.mult,
+                        )
+                    continue
                 dst = state[("o", g)][a // 2][:, h, i, :]
                 src = es[a // 2][:, h, i, :]
                 col = rs[:, c : c + 1]
@@ -266,48 +275,52 @@ def tile_multiheadattention_pb_t_kernel(tc, Q_bytes, Q_scale, WQ, out):
         junk = tp_pool.tile([P, K], F32, name="tp")
         for w in range(WARM_MATMULS):
             nc.tensor.matmul(out=junk[:], lhsT=idle[:, 0:P], rhs=idle[:], start=True, stop=True)
-        cast(0, HEAD_CASTS[0])
+        cast(0, "v")
         turn(0)
-        cast(1, HEAD_CASTS[1])
+        cast(1, "s")
         turn(1)
         state[("xb", -1)] = w_sb[:].rearrange("p r k -> p (r k)")
         turn(-1)
-        gather(0)
-        scale(0)
+        for g in range(2, LEAD + 1):
+            cast(g, "s")
+            turn(g)
+        for g in range(LEAD):
+            gather(g)
+            scale(g)
         group_weights()
-        cast(2, "s")
+        cast(LEAD + 1, "s")
 
         for it in range(0, n_groups + LAG + 1):
-            if ok(it + 1):
-                gather(it + 1)
-            if it == 0:
-                scale(1)
-                quantize(-1)
+            ahead = it + LEAD
+            if ok(ahead):
+                gather(ahead)
             if ok(it - LAG):
                 recip(it - LAG)
+            if it == 0:
+                quantize(-1)
             if ok(it):
                 quantize(it)
                 multiply(it)
             if ok(it - LAG - 1):
                 normalize(it - LAG - 1, "v")
                 store(it - LAG - 1)
-            if ok(it + 2):
-                turn(it + 2)
+            if ok(ahead + 1):
+                turn(ahead + 1)
             if ok(it - LAG):
                 normalize(it - LAG, "g", 0, FRONT)
-            if big(it + 1):
-                scale_gpsimd(it + 1)
+            if big(ahead):
+                scale_gpsimd(ahead)
             if ok(it - LAG):
                 normalize(it - LAG, "g", FRONT, 8)
             if ok(it - 1):
                 exps(it - 1)
             if ok(it - LAG):
                 normalize(it - LAG, "s")
-            if ok(it + 3):
-                cast(it + 3, "s")
-            if big(it + 2):
-                copy_words(it + 2)
-            if ok(it + 1) and it > 0:
-                scale(it + 1)
+            if ok(ahead + 2):
+                cast(ahead + 2, "s")
+            if big(ahead + 1):
+                copy_words(ahead + 1)
+            if ok(ahead):
+                scale(ahead)
             if ok(it):
                 maxima(it)

@@ -36,6 +36,7 @@ SHARE = {1: "gg", 2: "gggg", 4: "ggggssss"}
 TAIL_GROUPS = 3
 TAIL_SHARE = {1: "sv", 2: "svvg", 4: "gsgsgsgs"}
 WARM_MATMULS = 4
+DUMMY = 256
 
 
 def tile_multiheadattention_pb_t_kernel(tc, Q_bytes, Q_scale, WQ, out):
@@ -77,6 +78,8 @@ def tile_multiheadattention_pb_t_kernel(tc, Q_bytes, Q_scale, WQ, out):
         nc.vector.memset(zero[:], 0.0)
         idle = const.tile([P, K], BF16, name="idle")
         nc.vector.memset(idle[:], 0.0)
+        still = const.tile([P, DUMMY], F32, name="still")
+        nc.vector.memset(still[:], 0.0)
         nc.scalar.activation(out=warm[:], in_=zero[:], func=ACT.Exp)
         ident = const.tile([P, P], F32, name="ident")
         make_identity(nc, ident[:])
@@ -167,12 +170,21 @@ def tile_multiheadattention_pb_t_kernel(tc, Q_bytes, Q_scale, WQ, out):
             )
             state[("c", g)] = (codes, scl)
 
-        def multiply(g):
-            codes, scl = state[("c", g)]
-            w_codes, w_scl = state[("c", -1)]
+        def reserve(g):
             qps = []
             for a, m in banks(GROUPS[g][1]):
                 qp = qp_pool.tile([P, 2, HEADS * DK], F32, name="qp")
+                qps.append(qp)
+            state[("qp", g)] = qps
+
+        def keep_busy(g):
+            bank = state[("qp", g)][0][:].rearrange("p i n -> p (i n)")
+            nc.tensor.matmul(out=bank[:, 0:DUMMY], lhsT=ident[:], rhs=still[:], start=True, stop=True)
+
+        def multiply(g):
+            codes, scl = state[("c", g)]
+            w_codes, w_scl = state[("c", -1)]
+            for (a, m), qp in zip(banks(GROUPS[g][1]), state[("qp", g)]):
                 for i in range(m):
                     c0 = P * (a + i)
                     nc.tensor.matmul_mx(
@@ -184,8 +196,6 @@ def tile_multiheadattention_pb_t_kernel(tc, Q_bytes, Q_scale, WQ, out):
                         start=True,
                         stop=True,
                     )
-                qps.append(qp)
-            state[("qp", g)] = qps
 
         def maxima(g):
             nm = st_pool.tile([P, 8], F32, name="nm")
@@ -289,6 +299,8 @@ def tile_multiheadattention_pb_t_kernel(tc, Q_bytes, Q_scale, WQ, out):
             scale(g)
         group_weights()
         cast(LEAD + 1, "s")
+        reserve(0)
+        keep_busy(0)
 
         for it in range(0, n_groups + LAG + 1):
             ahead = it + LEAD
@@ -314,6 +326,10 @@ def tile_multiheadattention_pb_t_kernel(tc, Q_bytes, Q_scale, WQ, out):
                 normalize(it - LAG, "g", FRONT, 8)
             if ok(it - 1):
                 exps(it - 1)
+            if ok(it + 1):
+                reserve(it + 1)
+            if big(it + 1):
+                keep_busy(it + 1)
             if ok(it - LAG):
                 normalize(it - LAG, "s")
             if ok(ahead + 2):

from contextlib import ExitStack

import concourse.mybir as mybir
from concourse.masks import make_identity

FLOPS = 2 * 8192 * 512 * 256

F32 = mybir.dt.float32
BF16 = mybir.dt.bfloat16
U32 = mybir.dt.uint32
U8 = mybir.dt.uint8
FP8 = mybir.dt.float8_e4m3fn
FP8X4 = mybir.dt.float8_e4m3fn_x4
ACT = mybir.ActivationFunctionType
ALU = mybir.AluOpType
AX = mybir.AxisListType

P = 128
K = 512
BATCH = 4
HEADS = 2
DK = 128
LOADS = 16
BLOCKS = 64
BW = K

FIRST_SIZES = [1, 1, 2]
LAST_SIZES = [2, 1, 1]
SIZES = FIRST_SIZES + [4] * ((BLOCKS - sum(FIRST_SIZES) - sum(LAST_SIZES)) // 4) + LAST_SIZES
GROUPS = [(sum(SIZES[:g]), SIZES[g]) for g in range(len(SIZES))]
GN = 144
LAG = 2
LEAD = 2
FRONT = 8
SHARE = {1: "gg", 2: "gggg", 4: "ggggssss"}
TAIL_GROUPS = 3
TAIL_SHARE = {1: "sv", 2: "svvg", 4: "gsgsgsgs"}
WARM_MATMULS = 4
DUMMY = 256


def tile_multiheadattention_pb_t_kernel(tc, Q_bytes, Q_scale, WQ, out):
    nc = tc.nc
    n_groups = len(GROUPS)
    with ExitStack() as ctx:
        const = ctx.enter_context(tc.tile_pool(name="const", bufs=1))
        bytes_pool = ctx.enter_context(tc.tile_pool(name="bytes_pool", bufs=LOADS))
        xb_pool = ctx.enter_context(tc.tile_pool(name="xb_pool", bufs=3))
        raw_pool = ctx.enter_context(tc.tile_pool(name="raw_pool", bufs=3))
        g_pool = ctx.enter_context(tc.tile_pool(name="g_pool", bufs=4))
        c_pool = ctx.enter_context(tc.tile_pool(name="c_pool", bufs=3))
        st_pool = ctx.enter_context(tc.tile_pool(name="st_pool", bufs=5))
        e_pool = ctx.enter_context(tc.tile_pool(name="e_pool", bufs=10))
        o_pool = ctx.enter_context(tc.tile_pool(name="o_pool", bufs=8))
        tp_pool = ctx.enter_context(tc.psum_pool(name="tp_pool", bufs=4))
        qp_pool = ctx.enter_context(tc.psum_pool(name="qp_pool", bufs=4))
        ctx.enter_context(tc.manual_schedule())

        s_col = const.tile([P, 4], F32, name="s_col")
        q_tiles = []
        w_sb = const.tile([P, 2, K], BF16, name="w_sb", align_bytes=64)
        for s in range(LOADS):
            b, sb = divmod(s, LOADS // BATCH)
            q_bytes_sb = bytes_pool.tile([P, 4 * K], U8, name="q_bytes_sb")
            src = Q_bytes[b].rearrange("(s p i) k -> s p (i k)", p=P, i=4)[sb]
            if s == 0:
                nc.sync.dma_start(out=q_bytes_sb[:, 0:K], in_=src[:, 0:K])
                nc.sync.dma_start(out=s_col[:], in_=Q_scale.rearrange("a b (p t) -> p (a b t)", t=4))
                nc.sync.dma_start(out=q_bytes_sb[:, K : 2 * K], in_=src[:, K : 2 * K])
                nc.sync.dma_start(out=q_bytes_sb[:, 2 * K : 4 * K], in_=src[:, 2 * K : 4 * K])
                nc.sync.dma_start(out=w_sb[:], in_=WQ.rearrange("(r p) k -> p r k", p=P))
            else:
                nc.sync.dma_start(out=q_bytes_sb[:], in_=src)
            q_tiles.append(q_bytes_sb)

        zero = const.tile([P, 1], F32, name="zero")
        warm = const.tile([P, 1], F32, name="warm")
        nc.vector.memset(zero[:], 0.0)
        idle = const.tile([P, K], BF16, name="idle")
        nc.vector.memset(idle[:], 0.0)
        still = const.tile([P, DUMMY], F32, name="still")
        nc.vector.memset(still[:], 0.0)
        nc.scalar.activation(out=warm[:], in_=zero[:], func=ACT.Exp)
        ident = const.tile([P, P], F32, name="ident")
        make_identity(nc, ident[:])

        state = {}

        def ok(g):
            return 0 <= g < n_groups

        def big(g):
            return ok(g) and GROUPS[g][1] == 4

        def banks(n):
            return [(a, min(2, n - a)) for a in range(0, n, 2)]

        def cast(g, engine):
            first, n = GROUPS[g]
            s, i = divmod(first, 4)
            xb = xb_pool.tile([P, 4 * BW], BF16, name="xb", align_bytes=64)
            src = q_tiles[s][:, BW * i : BW * (i + n)].bitcast(FP8)
            if engine == "v":
                nc.vector.tensor_copy(out=xb[:, 0 : BW * n], in_=src)
            else:
                nc.scalar.copy(out=xb[:, 0 : BW * n], in_=src)
            state[("xb", g)] = xb[:]

        def turn(g):
            n = 2 if g < 0 else GROUPS[g][1]
            words = state[("xb", g)].bitcast(F32)
            tps = []
            for a, m in banks(n):
                tp = tp_pool.tile([P, 2, 2, P], F32, name="tp")
                for i in range(m):
                    for u in range(2):
                        c0 = 256 * (a + i)
                        nc.tensor.transpose(tp[:, u, i, :], words[:, c0 + u : c0 + 256 : 2], ident[:])
                tps.append(tp)
            state[("tp", g)] = tps

        def group_weights():
            gt = const.tile([P, 2 * BW], BF16, name="w_gt", align_bytes=64)
            nc.scalar.copy(
                out=gt[:].bitcast(F32).rearrange("p (n u) -> p n u", u=2),
                in_=state[("tp", -1)][0][:].rearrange("p u i r -> p (i r) u"),
            )
            state[("g", -1)] = gt

        def gather(g):
            state[("g", g)] = g_pool.tile([P, 4 * BW], BF16, name="gt", align_bytes=64)

        def scale(g):
            gt = state[("g", g)]
            for (a, m), tp in zip(banks(GROUPS[g][1]), state[("tp", g)]):
                n = P * m - (GN if big(g) and a == 2 else 0)
                src = tp[:].rearrange("p u i r -> p u (i r)").bitcast(BF16)
                nc.vector.tensor_tensor(
                    out=gt[:, BW * a : BW * a + 4 * n].rearrange("p (n u e) -> p n u e", u=2, e=2),
                    in0=src.rearrange("p u (n e) -> p n u e", e=2)[:, 0:n],
                    in1=s_col[:].rearrange("p (u e) -> p u e", u=2).unsqueeze(1).to_broadcast([P, n, 2, 2]),
                    op=ALU.mult,
                )

        def copy_words(g):
            raw = raw_pool.tile([P, GN, 4], BF16, name="raw", align_bytes=64)
            nc.scalar.copy(
                out=raw[:].rearrange("p n t -> p (n t)").bitcast(F32).rearrange("p (n u) -> p n u", u=2),
                in_=state[("tp", g)][1][:].rearrange("p u i r -> p (i r) u")[:, 2 * P - GN : 2 * P, :],
            )
            state[("raw", g)] = raw

        def scale_gpsimd(g):
            nc.gpsimd.tensor_tensor(
                out=state[("g", g)][:, 4 * (BW - GN) : 4 * BW].rearrange("p (n t) -> p n t", t=4),
                in0=state[("raw", g)][:],
                in1=s_col[:].unsqueeze(1).to_broadcast([P, GN, 4]),
                op=ALU.mult,
            )

        def quantize(g):
            n = 2 if g < 0 else GROUPS[g][1]
            pool = const if g < 0 else c_pool
            codes = pool.tile([P, 4 * P], U32, name="w_codes" if g < 0 else "codes", align_bytes=64)
            scl = pool.tile([P, 4 * P], U8, name="w_scl" if g < 0 else "scl", align_bytes=64)
            nc.vector.quantize_mx(
                out=codes[:, 0 : P * n].bitcast(FP8X4),
                scales=scl[:, 0 : P * n],
                in_=state[("g", g)][:, 0 : BW * n],
            )
            state[("c", g)] = (codes, scl)

        def reserve(g):
            qps = []
            for a, m in banks(GROUPS[g][1]):
                qp = qp_pool.tile([P, 2, HEADS * DK], F32, name="qp")
                qps.append(qp)
            state[("qp", g)] = qps

        def keep_busy(g):
            bank = state[("qp", g)][0][:].rearrange("p i n -> p (i n)")
            nc.tensor.matmul(out=bank[:, 0:DUMMY], lhsT=ident[:], rhs=still[:], start=True, stop=True)

        def multiply(g):
            codes, scl = state[("c", g)]
            w_codes, w_scl = state[("c", -1)]
            for (a, m), qp in zip(banks(GROUPS[g][1]), state[("qp", g)]):
                for i in range(m):
                    c0 = P * (a + i)
                    nc.tensor.matmul_mx(
                        out=qp[:, i, :],
                        lhsT=codes[:, c0 : c0 + P].bitcast(FP8X4),
                        lhsT_scale=scl[:, c0 : c0 + P],
                        rhs=w_codes[:, 0:256].bitcast(FP8X4),
                        rhs_scale=w_scl[:, 0:256],
                        start=True,
                        stop=True,
                    )

        def maxima(g):
            nm = st_pool.tile([P, 8], F32, name="nm")
            for (a, m), qp in zip(banks(GROUPS[g][1]), state[("qp", g)]):
                nc.vector.tensor_reduce(
                    out=nm[:, 2 * a : 2 * (a + m)],
                    in_=qp[:, 0:m, :].rearrange("p i (h d) -> p (i h) d", h=HEADS),
                    axis=AX.X,
                    op=ALU.max,
                    negate=True,
                )
            state[("nm", g)] = nm

        def panels(g):
            return [(a, i, h) for a, m in banks(GROUPS[g][1]) for i in range(m) for h in range(HEADS)]

        def exps(g):
            qps = state[("qp", g)]
            nm = state[("nm", g)]
            sm = st_pool.tile([P, 8], F32, name="sm")
            es = []
            for a, m in banks(GROUPS[g][1]):
                e = e_pool.tile([P, HEADS, 2, DK], F32, name="e")
                es.append(e)
            for c, (a, i, h) in enumerate(panels(g)):
                nc.scalar.activation(
                    out=es[a // 2][:, h, i, :],
                    in_=qps[a // 2][:, i, DK * h : DK * (h + 1)],
                    func=ACT.Exp,
                    bias=nm[:, c : c + 1],
                    scale=1.0,
                    accum_out=sm[:, c : c + 1],
                )
            state[("e", g)] = (es, sm)

        def recip(g):
            es, sm = state[("e", g)]
            n = 2 * GROUPS[g][1]
            rs = st_pool.tile([P, 8], F32, name="rs")
            nc.vector.reciprocal(out=rs[:, 0:n], in_=sm[:, 0:n])
            state[("rs", g)] = rs
            os_ = []
            for a, m in banks(GROUPS[g][1]):
                o = o_pool.tile([P, HEADS, 2, DK], F32, name="o")
                os_.append(o)
            state[("o", g)] = os_

        def normalize(g, engine, lo=0, hi=8):
            es, sm = state[("e", g)]
            rs = state[("rs", g)]
            share = (TAIL_SHARE if g >= n_groups - TAIL_GROUPS else SHARE)[GROUPS[g][1]]
            for c, (a, i, h) in enumerate(panels(g)):
                if share[c] != engine or not lo <= c < hi:
                    continue
                if engine == "g" and len(share) == 8:
                    if c % 4 == 0:
                        nc.gpsimd.tensor_tensor(
                            out=state[("o", g)][a // 2][:],
                            in0=es[a // 2][:],
                            in1=rs[:, c : c + 4].rearrange("p (i h) -> p h i", h=HEADS).unsqueeze(3).to_broadcast([P, HEADS, 2, DK]),
                            op=ALU.mult,
                        )
                    continue
                dst = state[("o", g)][a // 2][:, h, i, :]
                src = es[a // 2][:, h, i, :]
                col = rs[:, c : c + 1]
                if engine == "s":
                    nc.scalar.activation(out=dst, in_=src, func=ACT.Copy, scale=col)
                elif engine == "v":
                    nc.vector.tensor_scalar(out=dst, in0=src, scalar1=col, scalar2=None, op0=ALU.mult)
                else:
                    nc.gpsimd.tensor_scalar(
                        out=dst, in0=src, scalar1=col, scalar2=0.0, op0=ALU.mult, op1=ALU.add
                    )

        def store(g):
            first, n = GROUPS[g]
            for (a, m), o in zip(banks(n), state[("o", g)]):
                s, i = divmod(first + a, 4)
                b, sb = divmod(s, LOADS // BATCH)
                dst = out[b].rearrange("h (s p i) d -> s p h (i d)", p=P, i=4)[sb]
                nc.sync.dma_start(
                    out=dst[:, :, DK * i : DK * (i + m)],
                    in_=o[:, :, 0:m, :].rearrange("p h i d -> p h (i d)"),
                )

        junk = tp_pool.tile([P, K], F32, name="tp")
        for w in range(WARM_MATMULS):
            nc.tensor.matmul(out=junk[:], lhsT=idle[:, 0:P], rhs=idle[:], start=True, stop=True)
        cast(0, "v")
        turn(0)
        cast(1, "s")
        turn(1)
        state[("xb", -1)] = w_sb[:].rearrange("p r k -> p (r k)")
        turn(-1)
        for g in range(2, LEAD + 1):
            cast(g, "s")
            turn(g)
        for g in range(LEAD):
            gather(g)
            scale(g)
        group_weights()
        cast(LEAD + 1, "s")
        reserve(0)
        keep_busy(0)

        for it in range(0, n_groups + LAG + 1):
            ahead = it + LEAD
            if ok(ahead):
                gather(ahead)
            if ok(it - LAG):
                recip(it - LAG)
            if it == 0:
                quantize(-1)
            if ok(it):
                quantize(it)
                multiply(it)
            if ok(it - LAG - 1):
                normalize(it - LAG - 1, "v")
                store(it - LAG - 1)
            if ok(ahead + 1):
                turn(ahead + 1)
            if ok(it - LAG):
                normalize(it - LAG, "g", 0, FRONT)
            if big(ahead):
                scale_gpsimd(ahead)
            if ok(it - LAG):
                normalize(it - LAG, "g", FRONT, 8)
            if ok(it - 1):
                exps(it - 1)
            if ok(it + 1):
                reserve(it + 1)
            if big(it + 1):
                keep_busy(it + 1)
            if ok(it - LAG):
                normalize(it - LAG, "s")
            if ok(ahead + 2):
                cast(ahead + 2, "s")
            if big(ahead + 1):
                copy_words(ahead + 1)
            if ok(ahead):
                scale(ahead)
            if ok(it):
                maxima(it)
